import numpy as np
import ml_dtypes


def mxq(x, axis, fmt="e4m3"):
    dtype, down = {"e4m3": (ml_dtypes.float8_e4m3fn, 7), "e5m2": (ml_dtypes.float8_e5m2, 14)}[fmt]
    v = np.moveaxis(np.asarray(x, np.float32).astype(ml_dtypes.bfloat16).astype(np.float64), axis, -1)
    blocks = v.reshape(v.shape[:-1] + (-1, 32))
    amax = np.abs(blocks).max(-1, keepdims=True)
    byte = np.maximum(np.where(amax > 0, np.frexp(amax)[1] - 1 + 127, 0) - down, 1)
    scale = np.exp2(byte - 127.0)
    codes = (blocks / scale).astype(np.float32).astype(dtype).astype(np.float64)
    return np.moveaxis((codes * scale).reshape(v.shape), -1, axis)


WIDE = False


def mx_kscale(k):
    if not WIDE:
        return np.ones(k)
    levels = np.array([10, -10, 5, -5, 0])
    if k % 512:
        return np.exp2(np.random.permutation(np.resize(levels, k // 32))).repeat(32)
    a = np.empty((k // 512, 16))
    for p in range(k // 512):
        a[p, :8] = np.random.permutation(np.resize(levels, 8))
        for g in range(8):
            far = levels[np.abs(levels - a[p, g]) >= 10]
            a[p, g + 8] = far[np.random.randint(len(far))]
    return np.exp2(a.ravel()).repeat(32)


BF16 = ml_dtypes.bfloat16


def bf(x):
    return np.asarray(x, np.float32).astype(BF16)


def f64(x):
    return np.asarray(x).astype(np.float64)


B, H, W, C, NH, WS, SHIFT, F = 8, 32, 32, 2048, 64, 8, 3, 2048
S = WS * WS
HD = C // NH
NWIN = B * (H // WS) * (W // WS)
EPS = 1e-5


def layer_norm(x, w, b):
    m = x.mean(-1, keepdims=True)
    v = ((x - m) ** 2).mean(-1, keepdims=True)
    return (x - m) / np.sqrt(v + EPS) * w + b


def erf(z):
    a = np.clip(z, -6.0, 6.0)
    t2 = 2.0 * a * a
    term = a.copy()
    tot = a.copy()
    for n in range(1, 110):
        term = term * t2 / (2 * n + 1)
        tot = tot + term
    return 2.0 / np.sqrt(np.pi) * np.exp(-a * a) * tot


def gelu(v):
    return 0.5 * v * (1.0 + erf(v / np.sqrt(2.0)))


def setup_inputs():
    s = mx_kscale(C)
    t = mx_kscale(C)
    return {"o_heads": bf(0.25 * np.random.standard_normal((NWIN, NH, S, HD)) * s.reshape(NH, 1, HD)),
            "x": bf(np.random.standard_normal((B, H * W, C))),
            "out_w": bf(2.0 * np.random.standard_normal((C, C)) / np.sqrt(C) / s[None, :]),
            "out_b": bf(0.1 * np.random.standard_normal(C)),
            "norm2_w": bf((1.0 + 0.1 * np.random.standard_normal(C)) * t),
            "norm2_b": bf(0.1 * np.random.standard_normal(C) * t),
            "fc1_w": bf(np.random.standard_normal((F, C)) / np.sqrt(C) / t[None, :]),
            "fc1_b": bf(0.1 * np.random.standard_normal(F))}


def reference(o_heads, x, out_w, out_b, norm2_w, norm2_b, fc1_w, fc1_b):
    o = f64(o_heads).transpose(0, 2, 1, 3).reshape(-1, S, C)
    o = (mxq(o, 2, "e4m3") @ mxq(f64(out_w), 1, "e4m3").T) + f64(out_b)
    o = o.reshape(B, H // WS, W // WS, WS, WS, C)
    o = o.transpose(0, 1, 3, 2, 4, 5).reshape(B, H, W, C)
    o = np.roll(o, (SHIFT, SHIFT), axis=(1, 2))
    x2 = f64(x) + o.reshape(B, H * W, C)
    h2 = layer_norm(x2, f64(norm2_w), f64(norm2_b))
    g = gelu((mxq(h2, 2, "e4m3") @ mxq(f64(fc1_w), 1, "e4m3").T) + f64(fc1_b))
    return x2, g

@@ -1,0 +1,427 @@
+from contextlib import ExitStack
+
+import concourse.mybir as mybir
+from concourse.masks import make_identity
+
+F32 = mybir.dt.float32
+BF16 = mybir.dt.bfloat16
+U32 = mybir.dt.uint32
+U8 = mybir.dt.uint8
+I32 = mybir.dt.int32
+FP8X4 = mybir.dt.float8_e4m3fn_x4
+ACT = mybir.ActivationFunctionType
+ALU = mybir.AluOpType
+
+P = 128
+C = 2048
+NPASS = 4
+NBANK = 4
+BANK = 512
+NT = 64
+NRAW = 10
+EPS = 1e-5
+
+FLOPS = 2 * 2 * 8192 * 2048 * 2048
+
+
+def tile_swintransformerblock_pb_l_kernel(
+    tc, o_heads, x, out_w, out_b, norm2_w, norm2_b, fc1_w, fc1_b, out_0, out_1
+):
+    nc = tc.nc
+
+    oh_q = o_heads.rearrange("(q w) a s d -> w q a (s d)", w=4)
+    oh_w = o_heads.rearrange("(b w) a s d -> w b a (s d)", w=16)
+    x_v = x.flatten_outer_dims().rearrange("(q s) c -> s q c", s=256)
+    x2_v = out_0.flatten_outer_dims().rearrange("(q s) c -> s q c", s=256)
+    g_v = out_1.flatten_outer_dims().rearrange("(q s) c -> s q c", s=256)
+
+    with ExitStack() as ctx:
+        ctx.enter_context(tc.manual_schedule())
+        const = ctx.enter_context(tc.tile_pool(name="const", bufs=1))
+        lpool = ctx.enter_context(tc.tile_pool(name="lpool", bufs=2))
+        mpool = ctx.enter_context(tc.tile_pool(name="mpool", bufs=2))
+        xpool = ctx.enter_context(tc.tile_pool(name="xpool", bufs=2))
+        stat = ctx.enter_context(tc.tile_pool(name="stat", bufs=3))
+        mm_ps = ctx.enter_context(tc.psum_pool(name="mm_ps", bufs=4))
+        t_ps = ctx.enter_context(tc.psum_pool(name="t_ps", bufs=4))
+
+        ident = const.tile([P, P], F32, name="ident", tag="ident")
+        make_identity(nc, ident[:])
+        warm = const.tile([P, 8], F32, name="warm", tag="warm")
+        nc.vector.memset(warm[:], 0.0)
+        nc.scalar.activation(out=warm[:, 0:1], in_=warm[:, 1:2], func=ACT.Gelu)
+        mhalf = const.tile([P, 1], F32, name="mhalf", tag="mhalf")
+        nc.gpsimd.memset(mhalf[:], -0.5)
+
+        w_codes = []
+        w_planes = []
+        for s in range(2):
+            wc = const.tile([P, NPASS, C], U32, name="wc%d" % s, tag="wc%d" % s, align_bytes=64)
+            wp = const.tile([P, C], U8, name="wp%d" % s, tag="wp%d" % s, align_bytes=64)
+            nc.vector.memset(wp[:].bitcast(I32), 0)
+            w_codes.append(wc)
+            w_planes.append(wp)
+
+        nw_raw = const.tile([P, NPASS, 4], BF16, name="nw_raw", tag="nw_raw")
+        nb_raw = const.tile([P, NPASS, 4], BF16, name="nb_raw", tag="nb_raw")
+        nc.sync.dma_start(out=nw_raw[:], in_=norm2_w.rearrange("(g p t) -> p g t", g=NPASS, t=4))
+        nc.sync.dma_start(out=nb_raw[:], in_=norm2_b.rearrange("(g p t) -> p g t", g=NPASS, t=4))
+        nw_col = const.tile([P, NPASS * 4], F32, name="nw_col", tag="nw_col")
+        nb_col = const.tile([P, NPASS * 4], F32, name="nb_col", tag="nb_col")
+        nc.vector.tensor_copy(out=nw_col[:], in_=nw_raw[:].rearrange("p g t -> p (g t)"))
+        nc.vector.tensor_copy(out=nb_col[:], in_=nb_raw[:].rearrange("p g t -> p (g t)"))
+        ob = const.tile([P, C], BF16, name="ob", tag="ob")
+        fb = const.tile([P, C], BF16, name="fb", tag="fb")
+
+        live = {}
+
+        def load_l(q):
+            if q < 0 or q >= 8:
+                return
+            lt = lpool.tile([P, 64, 256], BF16, name="lt", tag="lt")
+            live[("l", q)] = lt
+            cols = slice(256 * q, 256 * q + 256)
+            if q < 5:
+                for wj in range(4):
+                    nc.sync.dma_start(out=lt[32 * wj : 32 * wj + 32, :, :], in_=oh_q[wj][:, :, cols])
+            else:
+                for ki in range(4):
+                    for wj in range(4):
+                        wi = (ki + 3) % 4
+                        nc.sync.dma_start(out=lt[32 * wj + ki : 32 * wj + 32 : 4, :, :], in_=oh_w[4 * wi + wj][:, :, cols])
+
+        def token_row(i, wj):
+            r, c = divmod(i, 8)
+            rho = r + 3 if r < 5 else r - 5
+            return 32 * rho + (8 * wj + c + 3) % 32
+
+        def load_x(i):
+            if i < 0 or i >= NT:
+                return
+            xt = xpool.tile([P, C], BF16, name="xt", tag="xt")
+            live[("x", i)] = xt
+            for wj in range(4):
+                nc.sync.dma_start(out=xt[32 * wj : 32 * wj + 32, :], in_=x_v[token_row(i, wj)])
+
+        def presort(i):
+            if i < 0 or i >= NT:
+                return
+            q, c = divmod(i, 8)
+            lw = live[("l", q)][:].bitcast(F32)
+            rt = mpool.tile([P, 2, 64, 8], F32, name="rt", tag="rt")
+            live[("r", i)] = rt
+            nc.vector.tensor_copy(
+                out=rt[:], in_=lw[:, :, 16 * c : 16 * c + 16].rearrange("p a (w u) -> p u a w", u=2)
+            )
+
+        def transposes8(src_of):
+            banks = []
+            for h in range(2):
+                bank = t_ps.tile([P, 2, 2, P], F32, name="tbank", tag="tbank")
+                for gg in range(2):
+                    for u in range(2):
+                        nc.tensor.transpose(bank[:, gg, u, :], src_of(2 * h + gg, u), ident[:])
+                banks.append(bank)
+            return banks
+
+        def tm(i):
+            if i < 0 or i >= NT:
+                return
+            rt = live.get(("r", i))
+            live[("tm", i)] = transposes8(
+                lambda g, u: rt[:, u, 16 * g : 16 * g + 16, :].rearrange("p a w -> p (a w)")
+            )
+
+        def copy_out(banks, engines):
+            mg = mpool.tile([P, NPASS, P, 4], BF16, name="mg", tag="mg", align_bytes=64)
+            mgw = mg[:].rearrange("p g n t -> p (g n t)").bitcast(F32).rearrange("p (g n u) -> p g n u", g=NPASS, u=2)
+            for h in range(2):
+                src = banks[h][:].rearrange("p g u n -> p g n u")
+                dst = mgw[:, 2 * h : 2 * h + 2, :, :]
+                if engines[h] == "s":
+                    nc.scalar.copy(out=dst, in_=src)
+                else:
+                    nc.vector.tensor_copy(out=dst, in_=src)
+            return mg
+
+        def mcopy(i):
+            if i < 0 or i >= NT:
+                return
+            live[("mg", i)] = copy_out(live.get(("tm", i)), "ss")
+
+        def mquant(i):
+            if i < 0 or i >= NT:
+                return
+            mg = live.get(("mg", i))
+            mc = mpool.tile([P, NPASS * P], U32, name="mc", tag="mc", align_bytes=64)
+            ms = mpool.tile([P, NPASS * P], U8, name="ms", tag="ms", align_bytes=64)
+            nc.vector.quantize_mx(
+                out=mc[:].bitcast(FP8X4), scales=ms[:], in_=mg[:].rearrange("p g n t -> p (g n t)")
+            )
+            live[("mc", i)] = (mc, ms)
+
+        def w_src(k):
+            return (out_w, fc1_w)[k // 16][P * (k % 16) : P * (k % 16) + P, :]
+
+        def wquant(k):
+            mg = live.get(("wg", k))
+            s, ct = divmod(k, 16)
+            cols = slice(P * ct, P * ct + P)
+            for g in range(NPASS):
+                nc.vector.quantize_mx(
+                    out=w_codes[s][:, g, cols].bitcast(FP8X4),
+                    scales=w_planes[s][4 * g : P, cols],
+                    in_=mg[:, g, :, :].rearrange("p n t -> p (n t)"),
+                )
+
+        load_l(0)
+        with tc.tile_pool(name="rawp", bufs=NRAW) as rawp:
+
+            def wload(k):
+                raw = rawp.tile([P, C], BF16, name="raw", tag="raw")
+                nc.sync.dma_start(out=raw[:], in_=w_src(k))
+                live[("raw", k)] = raw
+
+            for k in range(NRAW):
+                wload(k)
+            for k in range(32):
+                words = live.get(("raw", k))[:].bitcast(F32)
+                banks = transposes8(lambda g, u: words[:, 256 * g + u : 256 * (g + 1) : 2])
+                live[("wg", k)] = copy_out(banks, "sv" if k % 2 == 1 else "ss")
+                if k + NRAW < 32:
+                    wload(k + NRAW)
+                if k >= 1:
+                    wquant(k - 1)
+            wquant(31)
+
+        nc.sync.dma_start(out=ob[:], in_=out_b.partition_broadcast(P))
+        nc.sync.dma_start(out=fb[:], in_=fc1_b.partition_broadcast(P))
+
+        work = ctx.enter_context(tc.tile_pool(name="work", bufs=1))
+
+        def xb(i):
+            if i < 0 or i >= NT:
+                return
+            xt = live.get(("x", i))
+            x2t = xpool.tile([P, C], F32, name="x2t", tag="x2t")
+            live[("x2", i)] = x2t
+            for j in range(NBANK):
+                sl = slice(BANK * j, BANK * j + BANK)
+                nc.gpsimd.tensor_tensor(out=x2t[:, sl], in0=xt[:, sl], in1=ob[:, sl], op=ALU.add)
+
+        def mx_bank(codes, planes, s, j):
+            acc = mm_ps.tile([P, BANK], F32, name="acc", tag="acc")
+            sl = slice(BANK * j, BANK * j + BANK)
+            for g in range(NPASS):
+                gs = slice(P * g, P * g + P)
+                nc.tensor.matmul_mx(
+                    out=acc[:],
+                    lhsT=codes[:, gs].bitcast(FP8X4),
+                    lhsT_scale=planes[:, gs],
+                    rhs=w_codes[s][:, g, sl].bitcast(FP8X4),
+                    rhs_scale=w_planes[s][4 * g : P, sl],
+                    start=(g == 0),
+                    stop=(g == NPASS - 1),
+                )
+            return acc
+
+        def s1(i, j):
+            if i < 0 or i >= NT:
+                return
+            mc, ms = live[("mc", i)]
+            live[("p1", i, j)] = mx_bank(mc, ms, 0, j)
+
+        def x2evac(i, j):
+            if i < 0 or i >= NT:
+                return
+            if j == 0:
+                live[("sums", i)] = stat.tile([P, NBANK], F32, name="sums", tag="sums")
+            acc = live.get(("p1", i, j))
+            x2t = live[("x2", i)]
+            sl = slice(BANK * j, BANK * j + BANK)
+            nc.vector.scalar_tensor_tensor(
+                out=x2t[:, sl],
+                in0=acc[:],
+                scalar=1.0,
+                in1=x2t[:, sl],
+                op0=ALU.mult,
+                op1=ALU.add,
+                accum_out=live[("sums", i)][:, j : j + 1],
+            )
+
+        def mean(i):
+            if i < 0 or i >= NT:
+                return
+            sums = live.get(("sums", i))
+            scr = stat.tile([P, NBANK], F32, name="scr", tag="scr")
+            negmean = stat.tile([P, 1], F32, name="negmean", tag="negmean")
+            nc.vector.tensor_scalar(
+                out=scr[:], in0=sums[:], scalar1=-1.0 / C, scalar2=None, op0=ALU.mult, op1=ALU.add,
+                accum_out=negmean[:],
+            )
+            live[("negmean", i)] = negmean
+
+        def x2store(i):
+            if i < 0 or i >= NT:
+                return
+            x2t = live[("x2", i)]
+            for wj in range(4):
+                nc.sync.dma_start(out=x2_v[token_row(i, wj)], in_=x2t[32 * wj : 32 * wj + 32, :])
+
+        def square(i):
+            if i < 0 or i >= NT:
+                return
+            junk = work.tile([P, C], BF16, name="junk", tag="junk")
+            ssq = stat.tile([P, 1], F32, name="ssq", tag="ssq")
+            nc.scalar.activation(
+                out=junk[:], in_=live[("x2", i)][:], func=ACT.Square, bias=live[("negmean", i)][:], scale=1.0,
+                accum_out=ssq[:],
+            )
+            live[("ssq", i)] = ssq
+
+        def rstd(i):
+            if i < 0 or i >= NT:
+                return
+            ve = stat.tile([P, 1], F32, name="ve", tag="ve")
+            rs = stat.tile([P, 1], F32, name="rs", tag="rs")
+            nc.gpsimd.tensor_scalar(
+                out=ve[:], in0=live.get(("ssq", i))[:], scalar1=1.0 / C, scalar2=EPS, op0=ALU.mult, op1=ALU.add
+            )
+            nc.gpsimd.tensor_tensor(out=rs[:], in0=ve[:], in1=mhalf[:], op=ALU.pow)
+            live[("rs", i)] = rs
+
+        def znorm(i):
+            if i < 0 or i >= NT:
+                return
+            x2t = live.get(("x2", i))
+            zt = work.tile([P, NPASS, 4, P], F32, name="zt", tag="zt")
+            live[("z", i)] = zt
+            negmean = live.get(("negmean", i))
+            rs = live.get(("rs", i))
+            for g in range(NPASS):
+                nc.vector.tensor_scalar(
+                    out=zt[:, g, :, :],
+                    in0=x2t[:, BANK * g : BANK * g + BANK].rearrange("n (p t) -> n t p", t=4),
+                    scalar1=negmean[:],
+                    scalar2=rs[:],
+                    op0=ALU.add,
+                    op1=ALU.mult,
+                )
+
+        def tz(i):
+            if i < 0 or i >= NT:
+                return
+            zt = live.get(("z", i))
+            for g in range(NPASS):
+                bank = t_ps.tile([P, 4, P], F32, name="tbank", tag="tbank")
+                for t in range(4):
+                    nc.tensor.transpose(bank[:, t, :], zt[:, g, t, :], ident[:])
+                live[("tz", i, g)] = bank
+
+        def affine(i, g):
+            if i < 0 or i >= NT:
+                return
+            bank = live.get(("tz", i, g))
+            ht = work.tile([P, 4, P], BF16, name="ht", tag="ht", bufs=4)
+            for t in range(4):
+                col = slice(4 * g + t, 4 * g + t + 1)
+                nc.scalar.activation(
+                    out=ht[:, t, :], in_=bank[:, t, :], func=ACT.Identity, bias=nb_col[:, col], scale=nw_col[:, col]
+                )
+            live[("ht", i, g)] = ht
+
+        def interleave(i, g):
+            if i < 0 or i >= NT:
+                return
+            ht = live.get(("ht", i, g))
+            hg = work.tile([P, P, 4], BF16, name="hg", tag="hg", bufs=4, align_bytes=64)
+            nc.vector.tensor_copy(out=hg[:], in_=ht[:].rearrange("p t n -> p n t"))
+            live[("hg", i, g)] = hg
+
+        def hquant(i, g):
+            if i < 0 or i >= NT:
+                return
+            if g == 0:
+                hc = work.tile([P, NPASS * P], U32, name="hc", tag="hc", bufs=2, align_bytes=64)
+                hs = work.tile([P, NPASS * P], U8, name="hs", tag="hs", bufs=2, align_bytes=64)
+                live[("hc", i)] = (hc, hs)
+            hc, hs = live[("hc", i)]
+            gs = slice(P * g, P * g + P)
+            nc.vector.quantize_mx(
+                out=hc[:, gs].bitcast(FP8X4),
+                scales=hs[:, gs],
+                in_=live.get(("hg", i, g))[:].rearrange("p n t -> p (n t)"),
+            )
+
+        def s2(i, j):
+            if i < 0 or i >= NT:
+                return
+            hc, hs = live[("hc", i)]
+            live[("p2", i, j)] = mx_bank(hc, hs, 1, j)
+
+        def gevac(i, j):
+            if i < 0 or i >= NT:
+                return
+            if j == 0:
+                live[("g", i)] = work.tile([P, C], F32, name="gt", tag="gt", bufs=2)
+            sl = slice(BANK * j, BANK * j + BANK)
+            nc.vector.tensor_tensor(out=live[("g", i)][:, sl], in0=live.get(("p2", i, j))[:], in1=fb[:, sl], op=ALU.add)
+
+        def gelu(i, j):
+            if i < 0 or i >= NT:
+                return
+            sl = slice(BANK * j, BANK * j + BANK)
+            gt = live[("g", i)]
+            nc.scalar.activation(out=gt[:, sl], in_=gt[:, sl], func=ACT.Gelu)
+
+        def gstore(i):
+            if i < 0 or i >= NT:
+                return
+            gt = live.get(("g", i))
+            for wj in range(4):
+                nc.sync.dma_start(out=g_v[token_row(i, wj)], in_=gt[32 * wj : 32 * wj + 32, :])
+
+        for i in range(-2, NT + 2):
+            load_x(i + 2)
+            if (i + 2) % 8 == 0:
+                load_l((i + 2) // 8 + 1)
+            s1(i, 0)
+            znorm(i - 1)
+            xb(i + 1)
+            s1(i, 1)
+            x2evac(i, 0)
+            presort(i + 2)
+            s1(i, 2)
+            x2evac(i, 1)
+            mquant(i + 1)
+            s1(i, 3)
+            x2evac(i, 2)
+            tz(i - 1)
+            x2evac(i, 3)
+            mean(i)
+            x2store(i)
+            for g in range(NPASS):
+                affine(i - 1, g)
+            for j in range(NBANK):
+                s2(i - 2, j)
+            square(i)
+            rstd(i)
+            interleave(i - 1, 0)
+            interleave(i - 1, 1)
+            hquant(i - 1, 0)
+            interleave(i - 1, 2)
+            hquant(i - 1, 1)
+            gevac(i - 2, 0)
+            interleave(i - 1, 3)
+            hquant(i - 1, 2)
+            hquant(i - 1, 3)
+            gelu(i - 2, 0)
+            gevac(i - 2, 1)
+            gelu(i - 2, 1)
+            gevac(i - 2, 2)
+            gelu(i - 2, 2)
+            gevac(i - 2, 3)
+            gelu(i - 2, 3)
+            gstore(i - 2)
+            tm(i + 2)
+            mcopy(i + 2)

@@ -30,10 +30,9 @@ def tile_swintransformerblock_pb_l_kernel(
     nc = tc.nc
 
     oh_q = o_heads.rearrange("(q w) a s d -> w q a (s d)", w=4)
-    oh_w = o_heads.rearrange("(b w) a s d -> w b a (s d)", w=16)
-    x_v = x.flatten_outer_dims().rearrange("(q s) c -> s q c", s=256)
-    x2_v = out_0.flatten_outer_dims().rearrange("(q s) c -> s q c", s=256)
-    g_v = out_1.flatten_outer_dims().rearrange("(q s) c -> s q c", s=256)
+    x_v = x.flatten_outer_dims().rearrange("(p s) c -> s p c", s=64)
+    x2_v = out_0.flatten_outer_dims().rearrange("(p s) c -> s p c", s=64)
+    g_v = out_1.flatten_outer_dims().rearrange("(p s) c -> s p c", s=64)
 
     with ExitStack() as ctx:
         ctx.enter_context(tc.manual_schedule())
@@ -42,11 +41,19 @@ def tile_swintransformerblock_pb_l_kernel(
         mpool = ctx.enter_context(tc.tile_pool(name="mpool", bufs=2))
         xpool = ctx.enter_context(tc.tile_pool(name="xpool", bufs=2))
         stat = ctx.enter_context(tc.tile_pool(name="stat", bufs=3))
-        mm_ps = ctx.enter_context(tc.psum_pool(name="mm_ps", bufs=4))
-        t_ps = ctx.enter_context(tc.psum_pool(name="t_ps", bufs=4))
+        mm_ps = ctx.enter_context(tc.psum_pool(name="mm_ps", bufs=3))
+        t_ps = ctx.enter_context(tc.psum_pool(name="t_ps", bufs=5))
 
         ident = const.tile([P, P], F32, name="ident", tag="ident")
         make_identity(nc, ident[:])
+        perms = []
+        for sh in (1, 2):
+            perm = const.tile([P, P], F32, name="perm%d" % sh, tag="perm%d" % sh)
+            pv = perm[:].rearrange("k (b v) -> k b v", v=16)
+            iv = ident[:].rearrange("k (b v) -> k b v", v=16)
+            nc.vector.tensor_copy(out=pv[:, :, sh:16], in_=iv[:, :, 0 : 16 - sh])
+            nc.vector.tensor_copy(out=pv[:, :, 0:sh], in_=iv[:, :, 16 - sh : 16])
+            perms.append(perm)
         warm = const.tile([P, 8], F32, name="warm", tag="warm")
         nc.vector.memset(warm[:], 0.0)
         nc.scalar.activation(out=warm[:, 0:1], in_=warm[:, 1:2], func=ACT.Gelu)
@@ -80,28 +87,22 @@ def tile_swintransformerblock_pb_l_kernel(
                 return
             lt = lpool.tile([P, 64, 256], BF16, name="lt", tag="lt")
             live[("l", q)] = lt
-            cols = slice(256 * q, 256 * q + 256)
-            if q < 5:
-                for wj in range(4):
-                    nc.sync.dma_start(out=lt[32 * wj : 32 * wj + 32, :, :], in_=oh_q[wj][:, :, cols])
-            else:
-                for ki in range(4):
-                    for wj in range(4):
-                        wi = (ki + 3) % 4
-                        nc.sync.dma_start(out=lt[32 * wj + ki : 32 * wj + 32 : 4, :, :], in_=oh_w[4 * wi + wj][:, :, cols])
+            wj, par = divmod(q, 2)
+            for rr in range(4):
+                row = 2 * rr + par
+                nc.sync.dma_start(out=lt[rr:P:4, :, :], in_=oh_q[wj][:, :, 256 * row : 256 * row + 256])
 
-        def token_row(i, wj):
-            r, c = divmod(i, 8)
-            rho = r + 3 if r < 5 else r - 5
-            return 32 * rho + (8 * wj + c + 3) % 32
+        def token_row(i):
+            q, c = divmod(i, 8)
+            wj, par = divmod(q, 2)
+            return 32 * (1 - par) + (8 * wj + c + 3) % 32
 
         def load_x(i):
             if i < 0 or i >= NT:
                 return
             xt = xpool.tile([P, C], BF16, name="xt", tag="xt")
             live[("x", i)] = xt
-            for wj in range(4):
-                nc.sync.dma_start(out=xt[32 * wj : 32 * wj + 32, :], in_=x_v[token_row(i, wj)])
+            nc.sync.dma_start(out=xt[:], in_=x_v[token_row(i)])
 
         def presort(i):
             if i < 0 or i >= NT:
@@ -114,13 +115,13 @@ def tile_swintransformerblock_pb_l_kernel(
                 out=rt[:], in_=lw[:, :, 16 * c : 16 * c + 16].rearrange("p a (w u) -> p u a w", u=2)
             )
 
-        def transposes8(src_of):
+        def transposes8(src_of, ident_ap):
             banks = []
             for h in range(2):
                 bank = t_ps.tile([P, 2, 2, P], F32, name="tbank", tag="tbank")
                 for gg in range(2):
                     for u in range(2):
-                        nc.tensor.transpose(bank[:, gg, u, :], src_of(2 * h + gg, u), ident[:])
+                        nc.tensor.transpose(bank[:, gg, u, :], src_of(2 * h + gg, u), ident_ap)
                 banks.append(bank)
             return banks
 
@@ -129,7 +130,8 @@ def tile_swintransformerblock_pb_l_kernel(
                 return
             rt = live.get(("r", i))
             live[("tm", i)] = transposes8(
-                lambda g, u: rt[:, u, 16 * g : 16 * g + 16, :].rearrange("p a w -> p (a w)")
+                lambda g, u: rt[:, u, 16 * g : 16 * g + 16, :].rearrange("p a w -> p (a w)"),
+                perms[(i // 8) % 2][:],
             )
 
         def copy_out(banks, engines):
@@ -148,6 +150,15 @@ def tile_swintransformerblock_pb_l_kernel(
             if i < 0 or i >= NT:
                 return
             live[("mg", i)] = copy_out(live.get(("tm", i)), "ss")
+
+        def tz_one(i, g):
+            if i < 0 or i >= NT:
+                return
+            zt = live.get(("z", i))
+            bank = t_ps.tile([P, 4, P], F32, name="tbank", tag="tbank")
+            for t in range(4):
+                nc.tensor.transpose(bank[:, t, :], zt[:, g, t, :], ident[:])
+            live[("tz", i, g)] = bank
 
         def mquant(i):
             if i < 0 or i >= NT:
@@ -186,7 +197,7 @@ def tile_swintransformerblock_pb_l_kernel(
                 wload(k)
             for k in range(32):
                 words = live.get(("raw", k))[:].bitcast(F32)
-                banks = transposes8(lambda g, u: words[:, 256 * g + u : 256 * (g + 1) : 2])
+                banks = transposes8(lambda g, u: words[:, 256 * g + u : 256 * (g + 1) : 2], ident[:])
                 live[("wg", k)] = copy_out(banks, "sv" if k % 2 == 1 else "ss")
                 if k + NRAW < 32:
                     wload(k + NRAW)
@@ -265,8 +276,7 @@ def tile_swintransformerblock_pb_l_kernel(
             if i < 0 or i >= NT:
                 return
             x2t = live[("x2", i)]
-            for wj in range(4):
-                nc.sync.dma_start(out=x2_v[token_row(i, wj)], in_=x2t[32 * wj : 32 * wj + 32, :])
+            nc.sync.dma_start(out=x2_v[token_row(i)], in_=x2t[:])
 
         def square(i):
             if i < 0 or i >= NT:
@@ -378,50 +388,53 @@ def tile_swintransformerblock_pb_l_kernel(
             if i < 0 or i >= NT:
                 return
             gt = live.get(("g", i))
-            for wj in range(4):
-                nc.sync.dma_start(out=g_v[token_row(i, wj)], in_=gt[32 * wj : 32 * wj + 32, :])
+            nc.sync.dma_start(out=g_v[token_row(i)], in_=gt[:])
 
-        for i in range(-2, NT + 2):
+        for i in range(-2, NT + 3):
             load_x(i + 2)
             if (i + 2) % 8 == 0:
                 load_l((i + 2) // 8 + 1)
             s1(i, 0)
+            gevac(i - 3, 3)
+            gelu(i - 3, 0)
+            gelu(i - 3, 1)
+            gelu(i - 3, 2)
+            gelu(i - 3, 3)
+            gstore(i - 3)
             znorm(i - 1)
             xb(i + 1)
             s1(i, 1)
             x2evac(i, 0)
-            presort(i + 2)
             s1(i, 2)
             x2evac(i, 1)
-            mquant(i + 1)
             s1(i, 3)
             x2evac(i, 2)
-            tz(i - 1)
+            tm(i + 1)
+            tz_one(i - 1, 0)
+            tz_one(i - 1, 1)
+            tz_one(i - 1, 2)
+            mcopy(i + 1)
+            tz_one(i - 1, 3)
             x2evac(i, 3)
             mean(i)
             x2store(i)
+            presort(i + 2)
             for g in range(NPASS):
                 affine(i - 1, g)
-            for j in range(NBANK):
+            for j in range(NBANK - 1):
                 s2(i - 2, j)
             square(i)
             rstd(i)
+            mquant(i + 1)
             interleave(i - 1, 0)
             interleave(i - 1, 1)
             hquant(i - 1, 0)
+            gevac(i - 2, 0)
+            s2(i - 2, 3)
             interleave(i - 1, 2)
             hquant(i - 1, 1)
-            gevac(i - 2, 0)
             interleave(i - 1, 3)
-            hquant(i - 1, 2)
-            hquant(i - 1, 3)
-            gelu(i - 2, 0)
             gevac(i - 2, 1)
-            gelu(i - 2, 1)
+            hquant(i - 2 + 1, 2)
+            hquant(i - 1, 3)
             gevac(i - 2, 2)
-            gelu(i - 2, 2)
-            gevac(i - 2, 3)
-            gelu(i - 2, 3)
-            gstore(i - 2)
-            tm(i + 2)
-            mcopy(i + 2)

@@ -18,7 +18,7 @@ NPASS = 4
 NBANK = 4
 BANK = 512
 NT = 64
-NRAW = 10
+NRAW = 6
 EPS = 1e-5
 
 FLOPS = 2 * 2 * 8192 * 2048 * 2048
@@ -41,8 +41,9 @@ def tile_swintransformerblock_pb_l_kernel(
         mpool = ctx.enter_context(tc.tile_pool(name="mpool", bufs=2))
         xpool = ctx.enter_context(tc.tile_pool(name="xpool", bufs=2))
         stat = ctx.enter_context(tc.tile_pool(name="stat", bufs=3))
-        mm_ps = ctx.enter_context(tc.psum_pool(name="mm_ps", bufs=3))
-        t_ps = ctx.enter_context(tc.psum_pool(name="t_ps", bufs=5))
+        work = ctx.enter_context(tc.tile_pool(name="work", bufs=1))
+        late = {}
+        psum = ctx.enter_context(tc.psum_pool(name="psum", bufs=8))
 
         ident = const.tile([P, P], F32, name="ident", tag="ident")
         make_identity(nc, ident[:])
@@ -82,15 +83,18 @@ def tile_swintransformerblock_pb_l_kernel(
 
         live = {}
 
-        def load_l(q):
+        def load_l(q, parts):
             if q < 0 or q >= 8:
                 return
-            lt = lpool.tile([P, 64, 256], BF16, name="lt", tag="lt")
-            live[("l", q)] = lt
+            if ("l", q) not in live:
+                live[("l", q)] = lpool.tile([P, 64, 256], BF16, name="lt", tag="lt")
+            lt = live[("l", q)]
             wj, par = divmod(q, 2)
-            for rr in range(4):
+            for part in parts:
+                h, rr = divmod(part, 4)
                 row = 2 * rr + par
-                nc.sync.dma_start(out=lt[rr:P:4, :, :], in_=oh_q[wj][:, :, 256 * row : 256 * row + 256])
+                heads = slice(16 * h, 16 * h + 16)
+                nc.sync.dma_start(out=lt[rr:P:4, heads, :], in_=oh_q[wj][:, heads, 256 * row : 256 * row + 256])
 
         def token_row(i):
             q, c = divmod(i, 8)
@@ -111,14 +115,14 @@ def tile_swintransformerblock_pb_l_kernel(
             lw = live[("l", q)][:].bitcast(F32)
             rt = mpool.tile([P, 2, 64, 8], F32, name="rt", tag="rt")
             live[("r", i)] = rt
-            nc.vector.tensor_copy(
+            nc.scalar.copy(
                 out=rt[:], in_=lw[:, :, 16 * c : 16 * c + 16].rearrange("p a (w u) -> p u a w", u=2)
             )
 
         def transposes8(src_of, ident_ap):
             banks = []
             for h in range(2):
-                bank = t_ps.tile([P, 2, 2, P], F32, name="tbank", tag="tbank")
+                bank = psum.tile([P, 2, 2, P], F32, name="bank", tag="bank")
                 for gg in range(2):
                     for u in range(2):
                         nc.tensor.transpose(bank[:, gg, u, :], src_of(2 * h + gg, u), ident_ap)
@@ -155,7 +159,7 @@ def tile_swintransformerblock_pb_l_kernel(
             if i < 0 or i >= NT:
                 return
             zt = live.get(("z", i))
-            bank = t_ps.tile([P, 4, P], F32, name="tbank", tag="tbank")
+            bank = psum.tile([P, 4, P], F32, name="bank", tag="bank")
             for t in range(4):
                 nc.tensor.transpose(bank[:, t, :], zt[:, g, t, :], ident[:])
             live[("tz", i, g)] = bank
@@ -185,30 +189,20 @@ def tile_swintransformerblock_pb_l_kernel(
                     in_=mg[:, g, :, :].rearrange("p n t -> p (n t)"),
                 )
 
-        load_l(0)
-        with tc.tile_pool(name="rawp", bufs=NRAW) as rawp:
+        def wload(k):
+            if k >= 32:
+                return
+            raw = late["rawp"].tile([P, C], BF16, name="raw", tag="raw")
+            nc.sync.dma_start(out=raw[:], in_=w_src(k))
+            live[("raw", k)] = raw
 
-            def wload(k):
-                raw = rawp.tile([P, C], BF16, name="raw", tag="raw")
-                nc.sync.dma_start(out=raw[:], in_=w_src(k))
-                live[("raw", k)] = raw
-
-            for k in range(NRAW):
-                wload(k)
-            for k in range(32):
-                words = live.get(("raw", k))[:].bitcast(F32)
-                banks = transposes8(lambda g, u: words[:, 256 * g + u : 256 * (g + 1) : 2], ident[:])
-                live[("wg", k)] = copy_out(banks, "sv" if k % 2 == 1 else "ss")
-                if k + NRAW < 32:
-                    wload(k + NRAW)
-                if k >= 1:
-                    wquant(k - 1)
-            wquant(31)
-
-        nc.sync.dma_start(out=ob[:], in_=out_b.partition_broadcast(P))
-        nc.sync.dma_start(out=fb[:], in_=fc1_b.partition_broadcast(P))
-
-        work = ctx.enter_context(tc.tile_pool(name="work", bufs=1))
+        def wstep(k):
+            words = live.get(("raw", k))[:].bitcast(F32)
+            banks = transposes8(lambda g, u: words[:, 256 * g + u : 256 * (g + 1) : 2], ident[:])
+            live[("wg", k)] = copy_out(banks, "sv" if k % 2 == 1 else "ss")
+            wload(k + NRAW)
+            if k not in (0, NRAW, 16, 24):
+                wquant(k - 1)
 
         def xb(i):
             if i < 0 or i >= NT:
@@ -221,7 +215,7 @@ def tile_swintransformerblock_pb_l_kernel(
                 nc.gpsimd.tensor_tensor(out=x2t[:, sl], in0=xt[:, sl], in1=ob[:, sl], op=ALU.add)
 
         def mx_bank(codes, planes, s, j):
-            acc = mm_ps.tile([P, BANK], F32, name="acc", tag="acc")
+            acc = psum.tile([P, BANK], F32, name="bank", tag="bank")
             sl = slice(BANK * j, BANK * j + BANK)
             for g in range(NPASS):
                 gs = slice(P * g, P * g + P)
@@ -308,22 +302,21 @@ def tile_swintransformerblock_pb_l_kernel(
             live[("z", i)] = zt
             negmean = live.get(("negmean", i))
             rs = live.get(("rs", i))
-            for g in range(NPASS):
-                nc.vector.tensor_scalar(
-                    out=zt[:, g, :, :],
-                    in0=x2t[:, BANK * g : BANK * g + BANK].rearrange("n (p t) -> n t p", t=4),
-                    scalar1=negmean[:],
-                    scalar2=rs[:],
-                    op0=ALU.add,
-                    op1=ALU.mult,
-                )
+            nc.vector.tensor_scalar(
+                out=zt[:],
+                in0=x2t[:].rearrange("n (g p t) -> n g t p", g=NPASS, t=4),
+                scalar1=negmean[:],
+                scalar2=rs[:],
+                op0=ALU.add,
+                op1=ALU.mult,
+            )
 
         def tz(i):
             if i < 0 or i >= NT:
                 return
             zt = live.get(("z", i))
             for g in range(NPASS):
-                bank = t_ps.tile([P, 4, P], F32, name="tbank", tag="tbank")
+                bank = psum.tile([P, 4, P], F32, name="bank", tag="bank")
                 for t in range(4):
                     nc.tensor.transpose(bank[:, t, :], zt[:, g, t, :], ident[:])
                 live[("tz", i, g)] = bank
@@ -373,7 +366,7 @@ def tile_swintransformerblock_pb_l_kernel(
             if i < 0 or i >= NT:
                 return
             if j == 0:
-                live[("g", i)] = work.tile([P, C], F32, name="gt", tag="gt", bufs=2)
+                live[("g", i)] = late["gpool"].tile([P, C], F32, name="gt", tag="gt")
             sl = slice(BANK * j, BANK * j + BANK)
             nc.vector.tensor_tensor(out=live[("g", i)][:, sl], in0=live.get(("p2", i, j))[:], in1=fb[:, sl], op=ALU.add)
 
@@ -390,10 +383,11 @@ def tile_swintransformerblock_pb_l_kernel(
             gt = live.get(("g", i))
             nc.sync.dma_start(out=g_v[token_row(i)], in_=gt[:])
 
-        for i in range(-2, NT + 3):
+        def period(i):
             load_x(i + 2)
-            if (i + 2) % 8 == 0:
-                load_l((i + 2) // 8 + 1)
+            if i >= 2:
+                step = (i + 1) % 8
+                load_l((i + 1) // 8 + 1, (2 * step, 2 * step + 1))
             s1(i, 0)
             gevac(i - 3, 3)
             gelu(i - 3, 0)
@@ -401,6 +395,7 @@ def tile_swintransformerblock_pb_l_kernel(
             gelu(i - 3, 2)
             gelu(i - 3, 3)
             gstore(i - 3)
+            presort(i + 1)
             znorm(i - 1)
             xb(i + 1)
             s1(i, 1)
@@ -412,13 +407,12 @@ def tile_swintransformerblock_pb_l_kernel(
             tm(i + 1)
             tz_one(i - 1, 0)
             tz_one(i - 1, 1)
-            tz_one(i - 1, 2)
             mcopy(i + 1)
+            tz_one(i - 1, 2)
             tz_one(i - 1, 3)
             x2evac(i, 3)
             mean(i)
             x2store(i)
-            presort(i + 2)
             for g in range(NPASS):
                 affine(i - 1, g)
             for j in range(NBANK - 1):
@@ -435,6 +429,55 @@ def tile_swintransformerblock_pb_l_kernel(
             hquant(i - 1, 1)
             interleave(i - 1, 3)
             gevac(i - 2, 1)
-            hquant(i - 2 + 1, 2)
+            hquant(i - 1, 2)
             hquant(i - 1, 3)
             gevac(i - 2, 2)
+            if i == 1:
+                for k in range(24, 32):
+                    wstep(k)
+                wquant(31)
+
+        with tc.tile_pool(name="rawp", bufs=NRAW) as rawp:
+            late["rawp"] = rawp
+            for k in range(NRAW):
+                wload(k)
+            load_l(0, range(16))
+            nc.sync.dma_start(out=ob[:], in_=out_b.partition_broadcast(P))
+            load_x(0)
+            for k in range(NRAW):
+                wstep(k)
+            wquant(NRAW - 1)
+            presort(0)
+            tm(0)
+            mcopy(0)
+            xb(0)
+            load_x(1)
+            nc.sync.dma_start(out=fb[:], in_=fc1_b.partition_broadcast(P))
+            mquant(0)
+            presort(1)
+            load_x(2)
+            for j in range(NBANK):
+                for k in range((6, 8, 11, 15)[j], (8, 11, 15, 18)[j]):
+                    if k == 16:
+                        wquant(15)
+                        tm(1)
+                        mcopy(1)
+                    wstep(k)
+                    if k == 16:
+                        mquant(1)
+                s1(0, j)
+                x2evac(0, j)
+                if j == 0:
+                    xb(1)
+            mean(0)
+            x2store(0)
+            square(0)
+            rstd(0)
+            for k in range(18, 24):
+                wstep(k)
+            wquant(23)
+            period(1)
+        load_l(1, range(6))
+        late["gpool"] = ctx.enter_context(tc.tile_pool(name="gpool", bufs=2))
+        for i in range(2, NT + 3):
+            period(i)

@@ -386,8 +386,8 @@ def tile_swintransformerblock_pb_l_kernel(
         def period(i):
             load_x(i + 2)
             if i >= 2:
-                step = (i + 1) % 8
-                load_l((i + 1) // 8 + 1, (2 * step, 2 * step + 1))
+                step = (i + 2) % 8
+                load_l((i + 2) // 8 + 1, (2 * step, 2 * step + 1))
             s1(i, 0)
             gevac(i - 3, 3)
             gelu(i - 3, 0)
@@ -395,7 +395,7 @@ def tile_swintransformerblock_pb_l_kernel(
             gelu(i - 3, 2)
             gelu(i - 3, 3)
             gstore(i - 3)
-            presort(i + 1)
+            presort(i + 2)
             znorm(i - 1)
             xb(i + 1)
             s1(i, 1)
@@ -473,11 +473,12 @@ def tile_swintransformerblock_pb_l_kernel(
             x2store(0)
             square(0)
             rstd(0)
+            presort(2)
             for k in range(18, 24):
                 wstep(k)
             wquant(23)
             period(1)
-        load_l(1, range(6))
+        load_l(1, range(8))
         late["gpool"] = ctx.enter_context(tc.tile_pool(name="gpool", bufs=2))
         for i in range(2, NT + 3):
             period(i)

@@ -19,6 +19,7 @@ NBANK = 4
 BANK = 512
 NT = 64
 NRAW = 6
+SKEW = 128
 EPS = 1e-5
 
 FLOPS = 2 * 2 * 8192 * 2048 * 2048
@@ -64,11 +65,11 @@ def tile_swintransformerblock_pb_l_kernel(
         w_codes = []
         w_planes = []
         for s in range(2):
-            wc = const.tile([P, NPASS, C], U32, name="wc%d" % s, tag="wc%d" % s, align_bytes=64)
-            wp = const.tile([P, C], U8, name="wp%d" % s, tag="wp%d" % s, align_bytes=64)
+            wc = const.tile([P, NPASS, C], U32, name="wc%d" % s, tag="wc%d" % s, align_bytes=256)
+            wp = const.tile([P, C + SKEW], U8, name="wp%d" % s, tag="wp%d" % s, align_bytes=256)
             nc.vector.memset(wp[:].bitcast(I32), 0)
             w_codes.append(wc)
-            w_planes.append(wp)
+            w_planes.append(wp[:, SKEW : SKEW + C])
 
         nw_raw = const.tile([P, NPASS, 4], BF16, name="nw_raw", tag="nw_raw")
         nb_raw = const.tile([P, NPASS, 4], BF16, name="nb_raw", tag="nb_raw")
@@ -168,8 +169,9 @@ def tile_swintransformerblock_pb_l_kernel(
             if i < 0 or i >= NT:
                 return
             mg = live.get(("mg", i))
-            mc = mpool.tile([P, NPASS * P], U32, name="mc", tag="mc", align_bytes=64)
-            ms = mpool.tile([P, NPASS * P], U8, name="ms", tag="ms", align_bytes=64)
+            mc = mpool.tile([P, NPASS * P], U32, name="mc", tag="mc", align_bytes=256)
+            ms = mpool.tile([P, NPASS * P + SKEW], U8, name="ms", tag="ms", align_bytes=256)
+            ms = ms[:, SKEW : SKEW + NPASS * P]
             nc.vector.quantize_mx(
                 out=mc[:].bitcast(FP8X4), scales=ms[:], in_=mg[:].rearrange("p g n t -> p (g n t)")
             )
@@ -345,9 +347,9 @@ def tile_swintransformerblock_pb_l_kernel(
             if i < 0 or i >= NT:
                 return
             if g == 0:
-                hc = work.tile([P, NPASS * P], U32, name="hc", tag="hc", bufs=2, align_bytes=64)
-                hs = work.tile([P, NPASS * P], U8, name="hs", tag="hs", bufs=2, align_bytes=64)
-                live[("hc", i)] = (hc, hs)
+                hc = work.tile([P, NPASS * P], U32, name="hc", tag="hc", bufs=2, align_bytes=256)
+                hs = work.tile([P, NPASS * P + SKEW], U8, name="hs", tag="hs", bufs=2, align_bytes=256)
+                live[("hc", i)] = (hc, hs[:, SKEW : SKEW + NPASS * P])
             hc, hs = live[("hc", i)]
             gs = slice(P * g, P * g + P)
             nc.vector.quantize_mx(
@@ -386,8 +388,8 @@ def tile_swintransformerblock_pb_l_kernel(
         def period(i):
             load_x(i + 2)
             if i >= 2:
-                step = (i + 2) % 8
-                load_l((i + 2) // 8 + 1, (2 * step, 2 * step + 1))
+                step = (i + 1) % 8
+                load_l((i + 1) // 8 + 1, (2 * step, 2 * step + 1))
             s1(i, 0)
             gevac(i - 3, 3)
             gelu(i - 3, 0)
@@ -395,7 +397,7 @@ def tile_swintransformerblock_pb_l_kernel(
             gelu(i - 3, 2)
             gelu(i - 3, 3)
             gstore(i - 3)
-            presort(i + 2)
+            presort(i + 1)
             znorm(i - 1)
             xb(i + 1)
             s1(i, 1)
@@ -473,12 +475,11 @@ def tile_swintransformerblock_pb_l_kernel(
             x2store(0)
             square(0)
             rstd(0)
-            presort(2)
             for k in range(18, 24):
                 wstep(k)
             wquant(23)
             period(1)
-        load_l(1, range(8))
+        load_l(1, range(6))
         late["gpool"] = ctx.enter_context(tc.tile_pool(name="gpool", bufs=2))
         for i in range(2, NT + 3):
             period(i)

from contextlib import ExitStack

import concourse.mybir as mybir
from concourse.masks import make_identity

F32 = mybir.dt.float32
BF16 = mybir.dt.bfloat16
U32 = mybir.dt.uint32
U8 = mybir.dt.uint8
I32 = mybir.dt.int32
FP8X4 = mybir.dt.float8_e4m3fn_x4
ACT = mybir.ActivationFunctionType
ALU = mybir.AluOpType

P = 128
C = 2048
NPASS = 4
NBANK = 4
BANK = 512
NT = 64
NRAW = 6
SKEW = 128
EPS = 1e-5

FLOPS = 2 * 2 * 8192 * 2048 * 2048


def tile_swintransformerblock_pb_l_kernel(
    tc, o_heads, x, out_w, out_b, norm2_w, norm2_b, fc1_w, fc1_b, out_0, out_1
):
    nc = tc.nc

    oh_q = o_heads.rearrange("(q w) a s d -> w q a (s d)", w=4)
    x_v = x.flatten_outer_dims().rearrange("(p s) c -> s p c", s=64)
    x2_v = out_0.flatten_outer_dims().rearrange("(p s) c -> s p c", s=64)
    g_v = out_1.flatten_outer_dims().rearrange("(p s) c -> s p c", s=64)

    with ExitStack() as ctx:
        ctx.enter_context(tc.manual_schedule())
        const = ctx.enter_context(tc.tile_pool(name="const", bufs=1))
        lpool = ctx.enter_context(tc.tile_pool(name="lpool", bufs=2))
        mpool = ctx.enter_context(tc.tile_pool(name="mpool", bufs=2))
        xpool = ctx.enter_context(tc.tile_pool(name="xpool", bufs=2))
        stat = ctx.enter_context(tc.tile_pool(name="stat", bufs=3))
        work = ctx.enter_context(tc.tile_pool(name="work", bufs=1))
        late = {}
        psum = ctx.enter_context(tc.psum_pool(name="psum", bufs=8))

        ident = const.tile([P, P], F32, name="ident", tag="ident")
        make_identity(nc, ident[:])
        perms = []
        for sh in (1, 2):
            perm = const.tile([P, P], F32, name="perm%d" % sh, tag="perm%d" % sh)
            pv = perm[:].rearrange("k (b v) -> k b v", v=16)
            iv = ident[:].rearrange("k (b v) -> k b v", v=16)
            nc.vector.tensor_copy(out=pv[:, :, sh:16], in_=iv[:, :, 0 : 16 - sh])
            nc.vector.tensor_copy(out=pv[:, :, 0:sh], in_=iv[:, :, 16 - sh : 16])
            perms.append(perm)
        warm = const.tile([P, 8], F32, name="warm", tag="warm")
        nc.vector.memset(warm[:], 0.0)
        nc.scalar.activation(out=warm[:, 0:1], in_=warm[:, 1:2], func=ACT.Gelu)
        mhalf = const.tile([P, 1], F32, name="mhalf", tag="mhalf")
        nc.gpsimd.memset(mhalf[:], -0.5)

        w_codes = []
        w_planes = []
        for s in range(2):
            wc = const.tile([P, NPASS, C], U32, name="wc%d" % s, tag="wc%d" % s, align_bytes=256)
            wp = const.tile([P, C + SKEW], U8, name="wp%d" % s, tag="wp%d" % s, align_bytes=256)
            nc.vector.memset(wp[:].bitcast(I32), 0)
            w_codes.append(wc)
            w_planes.append(wp[:, SKEW : SKEW + C])

        nw_raw = const.tile([P, NPASS, 4], BF16, name="nw_raw", tag="nw_raw")
        nb_raw = const.tile([P, NPASS, 4], BF16, name="nb_raw", tag="nb_raw")
        nc.sync.dma_start(out=nw_raw[:], in_=norm2_w.rearrange("(g p t) -> p g t", g=NPASS, t=4))
        nc.sync.dma_start(out=nb_raw[:], in_=norm2_b.rearrange("(g p t) -> p g t", g=NPASS, t=4))
        nw_col = const.tile([P, NPASS * 4], F32, name="nw_col", tag="nw_col")
        nb_col = const.tile([P, NPASS * 4], F32, name="nb_col", tag="nb_col")
        nc.vector.tensor_copy(out=nw_col[:], in_=nw_raw[:].rearrange("p g t -> p (g t)"))
        nc.vector.tensor_copy(out=nb_col[:], in_=nb_raw[:].rearrange("p g t -> p (g t)"))
        ob = const.tile([P, C], BF16, name="ob", tag="ob")
        fb = const.tile([P, C], BF16, name="fb", tag="fb")

        live = {}

        def load_l(q, parts):
            if q < 0 or q >= 8:
                return
            if ("l", q) not in live:
                live[("l", q)] = lpool.tile([P, 64, 256], BF16, name="lt", tag="lt")
            lt = live[("l", q)]
            wj, par = divmod(q, 2)
            for part in parts:
                h, rr = divmod(part, 4)
                row = 2 * rr + par
                heads = slice(16 * h, 16 * h + 16)
                nc.sync.dma_start(out=lt[rr:P:4, heads, :], in_=oh_q[wj][:, heads, 256 * row : 256 * row + 256])

        def token_row(i):
            q, c = divmod(i, 8)
            wj, par = divmod(q, 2)
            return 32 * (1 - par) + (8 * wj + c + 3) % 32

        def load_x(i):
            if i < 0 or i >= NT:
                return
            xt = xpool.tile([P, C], BF16, name="xt", tag="xt")
            live[("x", i)] = xt
            nc.sync.dma_start(out=xt[:], in_=x_v[token_row(i)])

        def presort(i):
            if i < 0 or i >= NT:
                return
            q, c = divmod(i, 8)
            lw = live[("l", q)][:].bitcast(F32)
            rt = mpool.tile([P, 2, 64, 8], F32, name="rt", tag="rt")
            live[("r", i)] = rt
            nc.scalar.copy(
                out=rt[:], in_=lw[:, :, 16 * c : 16 * c + 16].rearrange("p a (w u) -> p u a w", u=2)
            )

        def transposes8(src_of, ident_ap):
            banks = []
            for h in range(2):
                bank = psum.tile([P, 2, 2, P], F32, name="bank", tag="bank")
                for gg in range(2):
                    for u in range(2):
                        nc.tensor.transpose(bank[:, gg, u, :], src_of(2 * h + gg, u), ident_ap)
                banks.append(bank)
            return banks

        def tm(i):
            if i < 0 or i >= NT:
                return
            rt = live.get(("r", i))
            live[("tm", i)] = transposes8(
                lambda g, u: rt[:, u, 16 * g : 16 * g + 16, :].rearrange("p a w -> p (a w)"),
                perms[(i // 8) % 2][:],
            )

        def copy_out(banks, engines):
            mg = mpool.tile([P, NPASS, P, 4], BF16, name="mg", tag="mg", align_bytes=64)
            mgw = mg[:].rearrange("p g n t -> p (g n t)").bitcast(F32).rearrange("p (g n u) -> p g n u", g=NPASS, u=2)
            for h in range(2):
                src = banks[h][:].rearrange("p g u n -> p g n u")
                dst = mgw[:, 2 * h : 2 * h + 2, :, :]
                if engines[h] == "s":
                    nc.scalar.copy(out=dst, in_=src)
                else:
                    nc.vector.tensor_copy(out=dst, in_=src)
            return mg

        def mcopy(i):
            if i < 0 or i >= NT:
                return
            live[("mg", i)] = copy_out(live.get(("tm", i)), "ss")

        def tz_one(i, g):
            if i < 0 or i >= NT:
                return
            zt = live.get(("z", i))
            bank = psum.tile([P, 4, P], F32, name="bank", tag="bank")
            for t in range(4):
                nc.tensor.transpose(bank[:, t, :], zt[:, g, t, :], ident[:])
            live[("tz", i, g)] = bank

        def mquant(i):
            if i < 0 or i >= NT:
                return
            mg = live.get(("mg", i))
            mc = mpool.tile([P, NPASS * P], U32, name="mc", tag="mc", align_bytes=256)
            ms = mpool.tile([P, NPASS * P + SKEW], U8, name="ms", tag="ms", align_bytes=256)
            ms = ms[:, SKEW : SKEW + NPASS * P]
            nc.vector.quantize_mx(
                out=mc[:].bitcast(FP8X4), scales=ms[:], in_=mg[:].rearrange("p g n t -> p (g n t)")
            )
            live[("mc", i)] = (mc, ms)

        def w_src(k):
            return (out_w, fc1_w)[k // 16][P * (k % 16) : P * (k % 16) + P, :]

        def wquant(k):
            mg = live.get(("wg", k))
            s, ct = divmod(k, 16)
            cols = slice(P * ct, P * ct + P)
            for g in range(NPASS):
                nc.vector.quantize_mx(
                    out=w_codes[s][:, g, cols].bitcast(FP8X4),
                    scales=w_planes[s][4 * g : P, cols],
                    in_=mg[:, g, :, :].rearrange("p n t -> p (n t)"),
                )

        def wload(k):
            if k >= 32:
                return
            raw = late["rawp"].tile([P, C], BF16, name="raw", tag="raw")
            nc.sync.dma_start(out=raw[:], in_=w_src(k))
            live[("raw", k)] = raw

        def wstep(k):
            words = live.get(("raw", k))[:].bitcast(F32)
            banks = transposes8(lambda g, u: words[:, 256 * g + u : 256 * (g + 1) : 2], ident[:])
            live[("wg", k)] = copy_out(banks, "sv" if k % 2 == 1 else "ss")
            wload(k + NRAW)
            if k not in (0, NRAW, 16, 24):
                wquant(k - 1)

        def xb(i):
            if i < 0 or i >= NT:
                return
            xt = live.get(("x", i))
            x2t = xpool.tile([P, C], F32, name="x2t", tag="x2t")
            live[("x2", i)] = x2t
            for j in range(NBANK):
                sl = slice(BANK * j, BANK * j + BANK)
                nc.gpsimd.tensor_tensor(out=x2t[:, sl], in0=xt[:, sl], in1=ob[:, sl], op=ALU.add)

        def mx_bank(codes, planes, s, j):
            acc = psum.tile([P, BANK], F32, name="bank", tag="bank")
            sl = slice(BANK * j, BANK * j + BANK)
            for g in range(NPASS):
                gs = slice(P * g, P * g + P)
                nc.tensor.matmul_mx(
                    out=acc[:],
                    lhsT=codes[:, gs].bitcast(FP8X4),
                    lhsT_scale=planes[:, gs],
                    rhs=w_codes[s][:, g, sl].bitcast(FP8X4),
                    rhs_scale=w_planes[s][4 * g : P, sl],
                    start=(g == 0),
                    stop=(g == NPASS - 1),
                )
            return acc

        def s1(i, j):
            if i < 0 or i >= NT:
                return
            mc, ms = live[("mc", i)]
            live[("p1", i, j)] = mx_bank(mc, ms, 0, j)

        def x2evac(i, j):
            if i < 0 or i >= NT:
                return
            if j == 0:
                live[("sums", i)] = stat.tile([P, NBANK], F32, name="sums", tag="sums")
            acc = live.get(("p1", i, j))
            x2t = live[("x2", i)]
            sl = slice(BANK * j, BANK * j + BANK)
            nc.vector.scalar_tensor_tensor(
                out=x2t[:, sl],
                in0=acc[:],
                scalar=1.0,
                in1=x2t[:, sl],
                op0=ALU.mult,
                op1=ALU.add,
                accum_out=live[("sums", i)][:, j : j + 1],
            )

        def mean(i):
            if i < 0 or i >= NT:
                return
            sums = live.get(("sums", i))
            scr = stat.tile([P, NBANK], F32, name="scr", tag="scr")
            negmean = stat.tile([P, 1], F32, name="negmean", tag="negmean")
            nc.vector.tensor_scalar(
                out=scr[:], in0=sums[:], scalar1=-1.0 / C, scalar2=None, op0=ALU.mult, op1=ALU.add,
                accum_out=negmean[:],
            )
            live[("negmean", i)] = negmean

        def x2store(i):
            if i < 0 or i >= NT:
                return
            x2t = live[("x2", i)]
            nc.sync.dma_start(out=x2_v[token_row(i)], in_=x2t[:])

        def square(i):
            if i < 0 or i >= NT:
                return
            junk = work.tile([P, C], BF16, name="junk", tag="junk")
            ssq = stat.tile([P, 1], F32, name="ssq", tag="ssq")
            nc.scalar.activation(
                out=junk[:], in_=live[("x2", i)][:], func=ACT.Square, bias=live[("negmean", i)][:], scale=1.0,
                accum_out=ssq[:],
            )
            live[("ssq", i)] = ssq

        def rstd(i):
            if i < 0 or i >= NT:
                return
            ve = stat.tile([P, 1], F32, name="ve", tag="ve")
            rs = stat.tile([P, 1], F32, name="rs", tag="rs")
            nc.gpsimd.tensor_scalar(
                out=ve[:], in0=live.get(("ssq", i))[:], scalar1=1.0 / C, scalar2=EPS, op0=ALU.mult, op1=ALU.add
            )
            nc.gpsimd.tensor_tensor(out=rs[:], in0=ve[:], in1=mhalf[:], op=ALU.pow)
            live[("rs", i)] = rs

        def znorm(i):
            if i < 0 or i >= NT:
                return
            x2t = live.get(("x2", i))
            zt = work.tile([P, NPASS, 4, P], F32, name="zt", tag="zt")
            live[("z", i)] = zt
            negmean = live.get(("negmean", i))
            rs = live.get(("rs", i))
            nc.vector.tensor_scalar(
                out=zt[:],
                in0=x2t[:].rearrange("n (g p t) -> n g t p", g=NPASS, t=4),
                scalar1=negmean[:],
                scalar2=rs[:],
                op0=ALU.add,
                op1=ALU.mult,
            )

        def tz(i):
            if i < 0 or i >= NT:
                return
            zt = live.get(("z", i))
            for g in range(NPASS):
                bank = psum.tile([P, 4, P], F32, name="bank", tag="bank")
                for t in range(4):
                    nc.tensor.transpose(bank[:, t, :], zt[:, g, t, :], ident[:])
                live[("tz", i, g)] = bank

        def affine(i, g):
            if i < 0 or i >= NT:
                return
            bank = live.get(("tz", i, g))
            ht = work.tile([P, 4, P], BF16, name="ht", tag="ht", bufs=4)
            for t in range(4):
                col = slice(4 * g + t, 4 * g + t + 1)
                nc.scalar.activation(
                    out=ht[:, t, :], in_=bank[:, t, :], func=ACT.Identity, bias=nb_col[:, col], scale=nw_col[:, col]
                )
            live[("ht", i, g)] = ht

        def interleave(i, g):
            if i < 0 or i >= NT:
                return
            ht = live.get(("ht", i, g))
            hg = work.tile([P, P, 4], BF16, name="hg", tag="hg", bufs=4, align_bytes=64)
            nc.vector.tensor_copy(out=hg[:], in_=ht[:].rearrange("p t n -> p n t"))
            live[("hg", i, g)] = hg

        def hquant(i, g):
            if i < 0 or i >= NT:
                return
            if g == 0:
                hc = work.tile([P, NPASS * P], U32, name="hc", tag="hc", bufs=2, align_bytes=256)
                hs = work.tile([P, NPASS * P + SKEW], U8, name="hs", tag="hs", bufs=2, align_bytes=256)
                live[("hc", i)] = (hc, hs[:, SKEW : SKEW + NPASS * P])
            hc, hs = live[("hc", i)]
            gs = slice(P * g, P * g + P)
            nc.vector.quantize_mx(
                out=hc[:, gs].bitcast(FP8X4),
                scales=hs[:, gs],
                in_=live.get(("hg", i, g))[:].rearrange("p n t -> p (n t)"),
            )

        def s2(i, j):
            if i < 0 or i >= NT:
                return
            hc, hs = live[("hc", i)]
            live[("p2", i, j)] = mx_bank(hc, hs, 1, j)

        def gevac(i, j):
            if i < 0 or i >= NT:
                return
            if j == 0:
                live[("g", i)] = late["gpool"].tile([P, C], F32, name="gt", tag="gt")
            sl = slice(BANK * j, BANK * j + BANK)
            nc.vector.tensor_tensor(out=live[("g", i)][:, sl], in0=live.get(("p2", i, j))[:], in1=fb[:, sl], op=ALU.add)

        def gelu(i, j):
            if i < 0 or i >= NT:
                return
            sl = slice(BANK * j, BANK * j + BANK)
            gt = live[("g", i)]
            nc.scalar.activation(out=gt[:, sl], in_=gt[:, sl], func=ACT.Gelu)

        def gstore(i):
            if i < 0 or i >= NT:
                return
            gt = live.get(("g", i))
            nc.sync.dma_start(out=g_v[token_row(i)], in_=gt[:])

        def period(i):
            load_x(i + 2)
            if i >= 2:
                step = (i + 1) % 8
                load_l((i + 1) // 8 + 1, (2 * step, 2 * step + 1))
            s1(i, 0)
            gevac(i - 3, 3)
            gelu(i - 3, 0)
            gelu(i - 3, 1)
            gelu(i - 3, 2)
            gelu(i - 3, 3)
            gstore(i - 3)
            presort(i + 1)
            znorm(i - 1)
            xb(i + 1)
            s1(i, 1)
            x2evac(i, 0)
            s1(i, 2)
            x2evac(i, 1)
            s1(i, 3)
            x2evac(i, 2)
            tm(i + 1)
            tz_one(i - 1, 0)
            tz_one(i - 1, 1)
            mcopy(i + 1)
            tz_one(i - 1, 2)
            tz_one(i - 1, 3)
            x2evac(i, 3)
            mean(i)
            x2store(i)
            for g in range(NPASS):
                affine(i - 1, g)
            for j in range(NBANK - 1):
                s2(i - 2, j)
            square(i)
            rstd(i)
            mquant(i + 1)
            interleave(i - 1, 0)
            interleave(i - 1, 1)
            hquant(i - 1, 0)
            gevac(i - 2, 0)
            s2(i - 2, 3)
            interleave(i - 1, 2)
            hquant(i - 1, 1)
            interleave(i - 1, 3)
            gevac(i - 2, 1)
            hquant(i - 1, 2)
            hquant(i - 1, 3)
            gevac(i - 2, 2)
            if i == 1:
                for k in range(24, 32):
                    wstep(k)
                wquant(31)

        with tc.tile_pool(name="rawp", bufs=NRAW) as rawp:
            late["rawp"] = rawp
            for k in range(NRAW):
                wload(k)
            load_l(0, range(16))
            nc.sync.dma_start(out=ob[:], in_=out_b.partition_broadcast(P))
            load_x(0)
            for k in range(NRAW):
                wstep(k)
            wquant(NRAW - 1)
            presort(0)
            tm(0)
            mcopy(0)
            xb(0)
            load_x(1)
            nc.sync.dma_start(out=fb[:], in_=fc1_b.partition_broadcast(P))
            mquant(0)
            presort(1)
            load_x(2)
            for j in range(NBANK):
                for k in range((6, 8, 11, 15)[j], (8, 11, 15, 18)[j]):
                    if k == 16:
                        wquant(15)
                        tm(1)
                        mcopy(1)
                    wstep(k)
                    if k == 16:
                        mquant(1)
                s1(0, j)
                x2evac(0, j)
                if j == 0:
                    xb(1)
            mean(0)
            x2store(0)
            square(0)
            rstd(0)
            for k in range(18, 24):
                wstep(k)
            wquant(23)
            period(1)
        load_l(1, range(6))
        late["gpool"] = ctx.enter_context(tc.tile_pool(name="gpool", bufs=2))
        for i in range(2, NT + 3):
            period(i)
